import numpy as np
import ml_dtypes


def mxq(x, axis, fmt="e4m3"):
    dtype, down = {"e4m3": (ml_dtypes.float8_e4m3fn, 7), "e5m2": (ml_dtypes.float8_e5m2, 14)}[fmt]
    v = np.moveaxis(np.asarray(x, np.float32).astype(ml_dtypes.bfloat16).astype(np.float64), axis, -1)
    blocks = v.reshape(v.shape[:-1] + (-1, 32))
    amax = np.abs(blocks).max(-1, keepdims=True)
    byte = np.maximum(np.where(amax > 0, np.frexp(amax)[1] - 1 + 127, 0) - down, 1)
    scale = np.exp2(byte - 127.0)
    codes = (blocks / scale).astype(np.float32).astype(dtype).astype(np.float64)
    return np.moveaxis((codes * scale).reshape(v.shape), -1, axis)


WIDE = False


def mx_kscale(k):
    if not WIDE:
        return np.ones(k)
    levels = np.array([10, -10, 5, -5, 0])
    if k % 512:
        return np.exp2(np.random.permutation(np.resize(levels, k // 32))).repeat(32)
    a = np.empty((k // 512, 16))
    for p in range(k // 512):
        a[p, :8] = np.random.permutation(np.resize(levels, 8))
        for g in range(8):
            far = levels[np.abs(levels - a[p, g]) >= 10]
            a[p, g + 8] = far[np.random.randint(len(far))]
    return np.exp2(a.ravel()).repeat(32)


BF16 = ml_dtypes.bfloat16


def bf(x):
    return np.asarray(x, np.float32).astype(BF16)


def f64(x):
    return np.asarray(x).astype(np.float64)


B, S, H, HO, E = 4, 128, 1024, 1024, 8


def kahan_sum_last(x):
    s = np.zeros_like(x[..., 0])
    c = np.zeros_like(s)
    for i in range(x.shape[-1]):
        y = x[..., i] - c
        t = s + y
        c = (t - s) - y
        s = t
    return s


def draw0():
    s = mx_kscale(H)
    return {"hidden_states": bf(np.random.standard_normal((B, S, H)) * s),
            "op_logits": bf(np.random.standard_normal((B, S, E)) * 1.3),
            "We": bf(np.random.standard_normal((E, H, HO)) / np.sqrt(H) / s[None, :, None]),
            "be": bf(np.random.standard_normal((E, HO)) * 0.3)}


def core(hidden_states, op_logits, We, be):
    l = f64(op_logits)
    ex = np.exp(l - l.max(-1, keepdims=True))
    op_w = ex / ex.sum(-1, keepdims=True)
    prod = mxq(f64(hidden_states), 2, "e4m3")[:, None] @ mxq(f64(We), 1, "e4m3")[None]
    expert_out = prod.transpose(0, 2, 1, 3) + f64(be)
    weighted = expert_out * op_w[:, :, :, None]
    return kahan_sum_last(np.moveaxis(weighted, 2, -1))


def e4m3fn_bytes(y):
    return np.clip(np.asarray(y, np.float64), -448.0, 448.0).astype(np.float32).astype(ml_dtypes.float8_e4m3fn).view(np.uint8)


def e4m3fn_values(b):
    return np.asarray(b, np.uint8).view(ml_dtypes.float8_e4m3fn).astype(np.float64)


def setup_inputs():
    d = draw0()
    x0 = np.asarray(d['We']).astype(np.float64)
    s = (np.max(np.abs(x0), axis=(0, 2), keepdims=True) / 448.0).astype(np.float32)
    out = {}
    for k, v in d.items():
        if k == 'We':
            out['We_bytes'] = e4m3fn_bytes(x0 / s.astype(np.float64))
            out['We_scale'] = s
        else:
            out[k] = v
    return out


def reference(hidden_states, op_logits, We_bytes, We_scale, be):
    return core(hidden_states, op_logits, e4m3fn_values(We_bytes) * We_scale.astype(np.float64), be)

@@ -1,0 +1,226 @@
+from contextlib import ExitStack
+
+import concourse.mybir as mybir
+from concourse.masks import make_identity
+
+F32 = mybir.dt.float32
+BF16 = mybir.dt.bfloat16
+U32 = mybir.dt.uint32
+U8 = mybir.dt.uint8
+FP8 = mybir.dt.float8_e4m3fn
+FP8X4 = mybir.dt.float8_e4m3fn_x4
+ACT = mybir.ActivationFunctionType
+ALU = mybir.AluOpType
+AX = mybir.AxisListType
+
+P = 128
+MT = 4
+K = 1024
+G = 2
+T = 4
+NOUT = 1024
+NE = 8
+
+FLOPS = 2 * MT * P * K * NOUT * NE
+
+LAST_WIDTHS = (512, 256, 128, 128)
+CHUNKS = [(e, c0, 512) for e in range(NE - 1) for c0 in (0, 512)] + [(NE - 1, sum(LAST_WIDTHS[:i]), LAST_WIDTHS[i]) for i in range(len(LAST_WIDTHS))]
+NCH = len(CHUNKS)
+S_COLS = [64, 32, 48, 80, 48, 80, 96, 48, 48, 112, 64, 80, 144, 144, 320, 288, 336, 304]
+G_COLS = [208, 176, 176, 192, 176, 176, 192, 176, 176, 192, 176, 192, 192, 176, 192, 224, 176, 208]
+V_PLANES = [(3, 5, 6, 7), (3, 7), (), (), (), (), (), ()]
+WIDE_BUFS = 3
+X_AFTER = 3
+
+
+def tile_enhancedmathematicalreasoning_pa_kernel(tc, hidden_states, op_logits, We_bytes, We_scale, be, out):
+    nc = tc.nc
+    with ExitStack() as ctx:
+        ctx.enter_context(tc.manual_schedule())
+        const = ctx.enter_context(tc.tile_pool(name="const", bufs=1))
+        widep = ctx.enter_context(tc.tile_pool(name="widep", bufs=WIDE_BUFS))
+        grp = ctx.enter_context(tc.tile_pool(name="grp", bufs=3))
+        psum = ctx.enter_context(tc.psum_pool(name="psum", bufs=8))
+
+        warm = const.tile([P, 1], F32, name="warm")
+        be3 = const.tile([P, NOUT], BF16, name="be3")
+        wsplit = const.tile([P, MT, P], BF16, name="wsplit")
+        nc.vector.memset(warm[:], 0.0)
+        nc.vector.memset(be3[:], 0.0)
+        nc.vector.memset(wsplit[:], 0.0)
+        nc.scalar.activation(out=warm[:], in_=warm[:], func=ACT.Exp)
+        ident_f = const.tile([P, P], F32, name="ident_f")
+        ident_b = const.tile([P, P], BF16, name="ident_b")
+        make_identity(nc, ident_f[:])
+        make_identity(nc, ident_b[:])
+
+        wscale = const.tile([P, G, T], F32, name="wscale")
+        nc.sync.dma_start(out=wscale[:], in_=We_scale.rearrange("o (g p t) x -> p g (o t x)", p=P, t=T))
+        wbytes = [const.tile([P, G, T, NOUT], U8, name="wbytes%d" % e) for e in range(NE)]
+        wsrc = We_bytes.rearrange("e (g p t) n -> e g p t n", p=P, t=T)
+        for t in range(T):
+            nc.sync.dma_start(out=wbytes[0][:, 0, t, :], in_=wsrc[0, 0, :, t, :])
+        logits = const.tile([P, MT, NE], BF16, name="logits")
+        nc.sync.dma_start(out=logits[:], in_=op_logits.rearrange("b s e -> s b e"))
+        nc.sync.dma_start(out=wbytes[0][:, 1], in_=wsrc[0, 1])
+        x_sb = [const.tile([P, K], BF16, name="x_sb%d" % m) for m in range(MT)]
+        for i in range(2, 2 * NE):
+            if i == X_AFTER:
+                for m in range(MT):
+                    nc.sync.dma_start(out=x_sb[m][:], in_=hidden_states[m])
+                for r in range(3):
+                    nc.sync.dma_start(out=be3[NE * r : NE * (r + 1), :], in_=be)
+            nc.sync.dma_start(out=wbytes[i // 2][:, i % 2], in_=wsrc[i // 2, i % 2])
+
+        acc = const.tile([P, MT, NOUT], F32, name="acc")
+        op_w = const.tile([P, MT, NE], F32, name="op_w")
+        hgrouped = const.tile([P, G, MT * P, T], BF16, name="hgrouped", align_bytes=64)
+        hcodes = const.tile([P, G * MT * P], U32, name="hcodes", align_bytes=64)
+        hscales = const.tile([P, G * MT * P], U8, name="hscales", align_bytes=64)
+
+        wide = {}
+        grouped = {}
+        codes = {}
+        scales = {}
+        banks = {}
+
+        def widen(e, plane):
+            if e not in wide:
+                wide[e] = widep.tile([P, G, T, NOUT], BF16, name="wide")
+            g, t = divmod(plane, T)
+            src = wbytes[e][:, g, t, :].bitcast(FP8)
+            if plane in V_PLANES[e]:
+                nc.vector.tensor_scalar(out=wide[e][:, g, t, :], in0=src, scalar1=wscale[:, g, t : t + 1], scalar2=None, op0=ALU.mult)
+            else:
+                nc.scalar.activation(out=wide[e][:, g, t, :], in_=src, func=ACT.Copy, scale=wscale[:, g, t : t + 1])
+
+        def widen_planes(e, planes):
+            for plane in planes:
+                if plane not in V_PLANES[e]:
+                    widen(e, plane)
+            for plane in planes:
+                if plane in V_PLANES[e]:
+                    widen(e, plane)
+
+        def interleave(c, who):
+            e, c0, width = CHUNKS[c]
+            if c not in grouped:
+                grouped[c] = grp.tile([P, G, width, T], BF16, name="grouped", align_bytes=64)
+            g_cut = G_COLS[c] * width // 512
+            s_cut = width - S_COLS[c] * width // 512
+            n0, n1 = {"G": (0, g_cut), "V": (g_cut, s_cut), "S": (s_cut, width)}[who]
+            if n0 == n1:
+                return
+            src = wide[e][:, :, :, c0 + n0 : c0 + n1].rearrange("p g t n -> p g n t")
+            dst = grouped[c][:, :, n0:n1, :]
+            if who == "V":
+                nc.vector.tensor_copy(out=dst, in_=src)
+            elif who == "S":
+                nc.scalar.copy(out=dst, in_=src)
+            else:
+                tick = grp.tile([P, 1], F32, name="tick")
+                nc.vector.memset(tick[:], 1.0)
+                nc.gpsimd.tensor_scalar(out=dst, in0=src, scalar1=tick[:, 0:1], scalar2=0.0, op0=ALU.mult, op1=ALU.add)
+
+        def quantize(c):
+            width = CHUNKS[c][2]
+            codes[c] = grp.tile([P, G * width], U32, name="codes", align_bytes=64)
+            scales[c] = grp.tile([P, G * width], U8, name="scales", align_bytes=64)
+            nc.vector.quantize_mx(out=codes[c][:].bitcast(FP8X4), scales=scales[c][:], in_=grouped[c][:].rearrange("p g n t -> p (g n t)"))
+
+        def multiply(c):
+            width = CHUNKS[c][2]
+            banks[c] = []
+            for m in range(MT):
+                bank = psum.tile([P, width], F32, name="bank")
+                banks[c].append(bank)
+                for g in range(G):
+                    tok = slice(g * MT * P + m * P, g * MT * P + (m + 1) * P)
+                    col = slice(g * width, (g + 1) * width)
+                    nc.tensor.matmul_mx(out=bank[:], lhsT=hcodes[:, tok].bitcast(FP8X4), lhsT_scale=hscales[:, tok],
+                                        rhs=codes[c][:, col].bitcast(FP8X4), rhs_scale=scales[c][:, col], start=(g == 0), stop=(g == G - 1))
+
+        def combine(c):
+            e, c0, width = CHUNKS[c]
+            for m in range(MT):
+                part = acc[:, m, c0 : c0 + width]
+                nc.vector.scalar_tensor_tensor(out=part, in0=banks[c][m][:], scalar=op_w[:, m, e : e + 1], in1=part, op0=ALU.mult, op1=ALU.add)
+                if e == NE - 1:
+                    nc.sync.dma_start(out=out[m, :, c0 : c0 + width], in_=part)
+
+        widen(0, 0)
+        lmax = const.tile([P, MT], F32, name="lmax")
+        shifted = const.tile([P, MT, NE], F32, name="shifted")
+        expd = const.tile([P, MT, NE], F32, name="expd")
+        esum = const.tile([P, MT], F32, name="esum")
+        rsum = const.tile([P, MT], F32, name="rsum")
+        nc.vector.tensor_reduce(out=lmax[:], in_=logits[:], axis=AX.X, op=ALU.max)
+        nc.vector.tensor_tensor(out=shifted[:], in0=logits[:], in1=lmax[:].unsqueeze(2).to_broadcast([P, MT, NE]), op=ALU.subtract)
+        nc.scalar.activation(out=expd[:], in_=shifted[:], func=ACT.Exp)
+        widen(0, 1)
+        widen(0, 3)
+        nc.vector.tensor_reduce(out=esum[:], in_=expd[:], axis=AX.X, op=ALU.add)
+        nc.vector.reciprocal(out=rsum[:], in_=esum[:])
+        nc.vector.tensor_tensor(out=op_w[:], in0=expd[:], in1=rsum[:].unsqueeze(2).to_broadcast([P, MT, NE]), op=ALU.mult)
+        rest1 = const.tile([P, MT, NE], F32, name="rest1")
+        rest2 = const.tile([P, MT, NE], F32, name="rest2")
+        nc.vector.tensor_copy(out=wsplit[:, :, 0:NE], in_=op_w[:])
+        nc.vector.tensor_tensor(out=rest1[:], in0=op_w[:], in1=wsplit[:, :, 0:NE], op=ALU.subtract)
+        nc.vector.tensor_copy(out=wsplit[:, :, NE : 2 * NE], in_=rest1[:])
+        nc.vector.tensor_tensor(out=rest2[:], in0=rest1[:], in1=wsplit[:, :, NE : 2 * NE], op=ALU.subtract)
+        nc.vector.tensor_copy(out=wsplit[:, :, 2 * NE : 3 * NE], in_=rest2[:])
+        wT_ps = psum.tile([P, MT, P], BF16, name="bank")
+        for m in range(MT):
+            nc.tensor.transpose(wT_ps[:, m, :], wsplit[:, m, :], ident_b[:])
+        wT = const.tile([P, MT, P], BF16, name="wT")
+        widen_planes(0, (2, 4, 5, 6, 7))
+        nc.scalar.copy(out=wT[:], in_=wT_ps[:])
+
+        xt = []
+        bias_ps = []
+
+        def transpose_hidden():
+            for m in range(MT):
+                xt.append(psum.tile([P, G, 2, P], F32, name="bank"))
+                words = x_sb[m][:].bitcast(F32)
+                for g in range(G):
+                    for u in range(2):
+                        nc.tensor.transpose(xt[m][:, g, u, :], words[:, 256 * g + u : 256 * (g + 1) : 2], ident_f[:])
+
+        def bias_products(half):
+            for m in range(MT):
+                bias_ps.append(psum.tile([P, 512], F32, name="bank"))
+                nc.tensor.matmul(out=bias_ps[half * MT + m][:], lhsT=wT[:, m, :], rhs=be3[:, half * 512 : (half + 1) * 512], start=True, stop=True)
+
+        def empty_banks(c):
+            if c == -3:
+                for m in range(MT):
+                    nc.vector.tensor_copy(out=hgrouped[:, :, m * P : (m + 1) * P, :].rearrange("p g r t -> p g (r t)").bitcast(F32).rearrange("p g (r u) -> p g r u", u=2),
+                                          in_=xt[m][:].rearrange("p g u r -> p g r u"))
+            elif c < 0:
+                half = c + 2
+                for m in range(MT):
+                    nc.vector.tensor_copy(out=acc[:, m, half * 512 : (half + 1) * 512], in_=bias_ps[half * MT + m][:])
+            else:
+                combine(c)
+
+        transpose_hidden()
+        bias_products(0)
+        for j in range(-2, NCH + 1):
+            if 0 <= j + 1 < NCH:
+                interleave(j + 1, "S")
+            if j + 2 < NCH:
+                e, c0, width = CHUNKS[j + 2]
+                if e + 1 < NE:
+                    widen_planes(e + 1, range(G * T * c0 // NOUT, G * T * (c0 + width) // NOUT))
+            if j == -1:
+                bias_products(1)
+                nc.vector.quantize_mx(out=hcodes[:].bitcast(FP8X4), scales=hscales[:], in_=hgrouped[:].rearrange("p g r t -> p (g r t)"))
+            if 0 <= j < NCH:
+                quantize(j)
+                multiply(j)
+            if 0 <= j + 1 < NCH:
+                interleave(j + 1, "V")
+            if j + 2 < NCH:
+                interleave(j + 2, "G")
+            empty_banks(j - 1)

@@ -26,10 +26,11 @@ FLOPS = 2 * MT * P * K * NOUT * NE
 LAST_WIDTHS = (512, 256, 128, 128)
 CHUNKS = [(e, c0, 512) for e in range(NE - 1) for c0 in (0, 512)] + [(NE - 1, sum(LAST_WIDTHS[:i]), LAST_WIDTHS[i]) for i in range(len(LAST_WIDTHS))]
 NCH = len(CHUNKS)
-S_COLS = [64, 32, 48, 80, 48, 80, 96, 48, 48, 112, 64, 80, 144, 144, 320, 288, 336, 304]
-G_COLS = [208, 176, 176, 192, 176, 176, 192, 176, 176, 192, 176, 192, 192, 176, 192, 224, 176, 208]
-V_PLANES = [(3, 5, 6, 7), (3, 7), (), (), (), (), (), ()]
+S_COLS = [64] * 12 + [192] * 2 + [320] * 4
+G_COLS = [192] * NCH
+V_PLANES = [(2, 3, 5, 6, 7), (6, 7), (), (), (), (), (), ()]
 WIDE_BUFS = 3
+LAST_LEAD = 3
 X_AFTER = 3
 
 
@@ -40,6 +41,7 @@ def tile_enhancedmathematicalreasoning_pa_kernel(tc, hidden_states, op_logits, W
         const = ctx.enter_context(tc.tile_pool(name="const", bufs=1))
         widep = ctx.enter_context(tc.tile_pool(name="widep", bufs=WIDE_BUFS))
         grp = ctx.enter_context(tc.tile_pool(name="grp", bufs=3))
+        pair = ctx.enter_context(tc.tile_pool(name="pair", bufs=2))
         psum = ctx.enter_context(tc.psum_pool(name="psum", bufs=8))
 
         warm = const.tile([P, 1], F32, name="warm")
@@ -74,7 +76,7 @@ def tile_enhancedmathematicalreasoning_pa_kernel(tc, hidden_states, op_logits, W
 
         acc = const.tile([P, MT, NOUT], F32, name="acc")
         op_w = const.tile([P, MT, NE], F32, name="op_w")
-        hgrouped = const.tile([P, G, MT * P, T], BF16, name="hgrouped", align_bytes=64)
+        hgrouped = pair.tile([P, G, MT * P, T], BF16, name="grouped", align_bytes=64)
         hcodes = const.tile([P, G * MT * P], U32, name="hcodes", align_bytes=64)
         hscales = const.tile([P, G * MT * P], U8, name="hscales", align_bytes=64)
 
@@ -84,32 +86,42 @@ def tile_enhancedmathematicalreasoning_pa_kernel(tc, hidden_states, op_logits, W
         scales = {}
         banks = {}
 
-        def widen(e, plane):
+        def widen(e, plane, c0=0, width=NOUT):
             if e not in wide:
                 wide[e] = widep.tile([P, G, T, NOUT], BF16, name="wide")
             g, t = divmod(plane, T)
-            src = wbytes[e][:, g, t, :].bitcast(FP8)
+            src = wbytes[e][:, g, t, c0 : c0 + width].bitcast(FP8)
             if plane in V_PLANES[e]:
-                nc.vector.tensor_scalar(out=wide[e][:, g, t, :], in0=src, scalar1=wscale[:, g, t : t + 1], scalar2=None, op0=ALU.mult)
+                nc.vector.tensor_scalar(out=wide[e][:, g, t, c0 : c0 + width], in0=src, scalar1=wscale[:, g, t : t + 1], scalar2=None, op0=ALU.mult)
             else:
-                nc.scalar.activation(out=wide[e][:, g, t, :], in_=src, func=ACT.Copy, scale=wscale[:, g, t : t + 1])
+                nc.scalar.activation(out=wide[e][:, g, t, c0 : c0 + width], in_=src, func=ACT.Copy, scale=wscale[:, g, t : t + 1])
 
-        def widen_planes(e, planes):
+        def widen_planes(e, planes, c0=0, width=NOUT):
             for plane in planes:
                 if plane not in V_PLANES[e]:
-                    widen(e, plane)
+                    widen(e, plane, c0, width)
             for plane in planes:
                 if plane in V_PLANES[e]:
-                    widen(e, plane)
+                    widen(e, plane, c0, width)
+
+        def widen_for_step(j):
+            e = (j + 4) // 2
+            half = range(T * (j % 2), T * (j % 2) + T)
+            if 1 <= e < NE - 1:
+                widen_planes(e, half)
+            elif e == NE - 1:
+                widen_planes(e, half, 0, LAST_WIDTHS[0])
+            elif j + LAST_LEAD < NCH:
+                widen_planes(NE - 1, range(G * T), CHUNKS[j + LAST_LEAD][1], CHUNKS[j + LAST_LEAD][2])
 
         def interleave(c, who):
             e, c0, width = CHUNKS[c]
             if c not in grouped:
-                grouped[c] = grp.tile([P, G, width, T], BF16, name="grouped", align_bytes=64)
+                grouped[c] = pair.tile([P, G, width, T], BF16, name="grouped", align_bytes=64)
             g_cut = G_COLS[c] * width // 512
             s_cut = width - S_COLS[c] * width // 512
             n0, n1 = {"G": (0, g_cut), "V": (g_cut, s_cut), "S": (s_cut, width)}[who]
-            if n0 == n1:
+            if n0 >= n1:
                 return
             src = wide[e][:, :, :, c0 + n0 : c0 + n1].rearrange("p g t n -> p g n t")
             dst = grouped[c][:, :, n0:n1, :]
@@ -118,9 +130,7 @@ def tile_enhancedmathematicalreasoning_pa_kernel(tc, hidden_states, op_logits, W
             elif who == "S":
                 nc.scalar.copy(out=dst, in_=src)
             else:
-                tick = grp.tile([P, 1], F32, name="tick")
-                nc.vector.memset(tick[:], 1.0)
-                nc.gpsimd.tensor_scalar(out=dst, in0=src, scalar1=tick[:, 0:1], scalar2=0.0, op0=ALU.mult, op1=ALU.add)
+                nc.gpsimd.tensor_scalar(out=dst, in0=src, scalar1=1.0, scalar2=0.0, op0=ALU.mult, op1=ALU.add)
 
         def quantize(c):
             width = CHUNKS[c][2]
@@ -209,10 +219,7 @@ def tile_enhancedmathematicalreasoning_pa_kernel(tc, hidden_states, op_logits, W
         for j in range(-2, NCH + 1):
             if 0 <= j + 1 < NCH:
                 interleave(j + 1, "S")
-            if j + 2 < NCH:
-                e, c0, width = CHUNKS[j + 2]
-                if e + 1 < NE:
-                    widen_planes(e + 1, range(G * T * c0 // NOUT, G * T * (c0 + width) // NOUT))
+            widen_for_step(j)
             if j == -1:
                 bias_products(1)
                 nc.vector.quantize_mx(out=hcodes[:].bitcast(FP8X4), scales=hscales[:], in_=hgrouped[:].rearrange("p g r t -> p (g r t)"))

@@ -114,7 +114,7 @@ def tile_enhancedmathematicalreasoning_pa_kernel(tc, hidden_states, op_logits, W
             elif j + LAST_LEAD < NCH:
                 widen_planes(NE - 1, range(G * T), CHUNKS[j + LAST_LEAD][1], CHUNKS[j + LAST_LEAD][2])
 
-        def interleave(c, who):
+        def interleave(c, who, passes=(0, 1)):
             e, c0, width = CHUNKS[c]
             if c not in grouped:
                 grouped[c] = pair.tile([P, G, width, T], BF16, name="grouped", align_bytes=64)
@@ -123,14 +123,17 @@ def tile_enhancedmathematicalreasoning_pa_kernel(tc, hidden_states, op_logits, W
             n0, n1 = {"G": (0, g_cut), "V": (g_cut, s_cut), "S": (s_cut, width)}[who]
             if n0 >= n1:
                 return
-            src = wide[e][:, :, :, c0 + n0 : c0 + n1].rearrange("p g t n -> p g n t")
-            dst = grouped[c][:, :, n0:n1, :]
-            if who == "V":
-                nc.vector.tensor_copy(out=dst, in_=src)
-            elif who == "S":
-                nc.scalar.copy(out=dst, in_=src)
-            else:
-                nc.gpsimd.tensor_scalar(out=dst, in0=src, scalar1=1.0, scalar2=0.0, op0=ALU.mult, op1=ALU.add)
+            if who == "G":
+                src = wide[e][:, :, :, c0 + n0 : c0 + n1].rearrange("p g t n -> p g n t")
+                nc.gpsimd.tensor_scalar(out=grouped[c][:, :, n0:n1, :], in0=src, scalar1=1.0, scalar2=0.0, op0=ALU.mult, op1=ALU.add)
+                return
+            for g in passes:
+                src = wide[e][:, g, :, c0 + n0 : c0 + n1].rearrange("p t (c i) -> p c t i", i=4)
+                dst = grouped[c][:, g, n0:n1, :].rearrange("p (c i) t -> p c t i", i=4)
+                if who == "V":
+                    nc.vector.tensor_copy(out=dst, in_=src)
+                else:
+                    nc.scalar.copy(out=dst, in_=src)
 
         def quantize(c):
             width = CHUNKS[c][2]
@@ -220,6 +223,8 @@ def tile_enhancedmathematicalreasoning_pa_kernel(tc, hidden_states, op_logits, W
             if 0 <= j + 1 < NCH:
                 interleave(j + 1, "S")
             widen_for_step(j)
+            if 0 <= j + 1 < NCH:
+                interleave(j + 1, "V", (0,))
             if j == -1:
                 bias_products(1)
                 nc.vector.quantize_mx(out=hcodes[:].bitcast(FP8X4), scales=hscales[:], in_=hgrouped[:].rearrange("p g r t -> p (g r t)"))
@@ -227,7 +232,7 @@ def tile_enhancedmathematicalreasoning_pa_kernel(tc, hidden_states, op_logits, W
                 quantize(j)
                 multiply(j)
             if 0 <= j + 1 < NCH:
-                interleave(j + 1, "V")
+                interleave(j + 1, "V", (1,))
             if j + 2 < NCH:
                 interleave(j + 2, "G")
             empty_banks(j - 1)

@@ -26,9 +26,9 @@ FLOPS = 2 * MT * P * K * NOUT * NE
 LAST_WIDTHS = (512, 256, 128, 128)
 CHUNKS = [(e, c0, 512) for e in range(NE - 1) for c0 in (0, 512)] + [(NE - 1, sum(LAST_WIDTHS[:i]), LAST_WIDTHS[i]) for i in range(len(LAST_WIDTHS))]
 NCH = len(CHUNKS)
-S_COLS = [64] * 12 + [192] * 2 + [320] * 4
+S_COLS = [64] * 12 + [224] * 2 + [320] * (NCH - 14)
 G_COLS = [192] * NCH
-V_PLANES = [(2, 3, 5, 6, 7), (6, 7), (), (), (), (), (), ()]
+V_PLANES = [(2, 3, 5, 6, 7), (2, 3, 6), (), (), (), (), (), ()]
 WIDE_BUFS = 3
 LAST_LEAD = 3
 X_AFTER = 3
@@ -49,7 +49,6 @@ def tile_enhancedmathematicalreasoning_pa_kernel(tc, hidden_states, op_logits, W
         wsplit = const.tile([P, MT, P], BF16, name="wsplit")
         nc.vector.memset(warm[:], 0.0)
         nc.vector.memset(be3[:], 0.0)
-        nc.vector.memset(wsplit[:], 0.0)
         nc.scalar.activation(out=warm[:], in_=warm[:], func=ACT.Exp)
         ident_f = const.tile([P, P], F32, name="ident_f")
         ident_b = const.tile([P, P], BF16, name="ident_b")
@@ -85,8 +84,12 @@ def tile_enhancedmathematicalreasoning_pa_kernel(tc, hidden_states, op_logits, W
         codes = {}
         scales = {}
         banks = {}
+        widened = set()
 
         def widen(e, plane, c0=0, width=NOUT):
+            if (e, plane, c0) in widened:
+                return
+            widened.add((e, plane, c0))
             if e not in wide:
                 wide[e] = widep.tile([P, G, T, NOUT], BF16, name="wide")
             g, t = divmod(plane, T)
@@ -161,33 +164,36 @@ def tile_enhancedmathematicalreasoning_pa_kernel(tc, hidden_states, op_logits, W
                 if e == NE - 1:
                     nc.sync.dma_start(out=out[m, :, c0 : c0 + width], in_=part)
 
-        widen(0, 0)
         lmax = const.tile([P, MT], F32, name="lmax")
         shifted = const.tile([P, MT, NE], F32, name="shifted")
         expd = const.tile([P, MT, NE], F32, name="expd")
         esum = const.tile([P, MT], F32, name="esum")
         rsum = const.tile([P, MT], F32, name="rsum")
-        nc.vector.tensor_reduce(out=lmax[:], in_=logits[:], axis=AX.X, op=ALU.max)
-        nc.vector.tensor_tensor(out=shifted[:], in0=logits[:], in1=lmax[:].unsqueeze(2).to_broadcast([P, MT, NE]), op=ALU.subtract)
-        nc.scalar.activation(out=expd[:], in_=shifted[:], func=ACT.Exp)
-        widen(0, 1)
-        widen(0, 3)
-        nc.vector.tensor_reduce(out=esum[:], in_=expd[:], axis=AX.X, op=ALU.add)
-        nc.vector.reciprocal(out=rsum[:], in_=esum[:])
-        nc.vector.tensor_tensor(out=op_w[:], in0=expd[:], in1=rsum[:].unsqueeze(2).to_broadcast([P, MT, NE]), op=ALU.mult)
         rest1 = const.tile([P, MT, NE], F32, name="rest1")
         rest2 = const.tile([P, MT, NE], F32, name="rest2")
-        nc.vector.tensor_copy(out=wsplit[:, :, 0:NE], in_=op_w[:])
-        nc.vector.tensor_tensor(out=rest1[:], in0=op_w[:], in1=wsplit[:, :, 0:NE], op=ALU.subtract)
-        nc.vector.tensor_copy(out=wsplit[:, :, NE : 2 * NE], in_=rest1[:])
-        nc.vector.tensor_tensor(out=rest2[:], in0=rest1[:], in1=wsplit[:, :, NE : 2 * NE], op=ALU.subtract)
-        nc.vector.tensor_copy(out=wsplit[:, :, 2 * NE : 3 * NE], in_=rest2[:])
-        wT_ps = psum.tile([P, MT, P], BF16, name="bank")
-        for m in range(MT):
-            nc.tensor.transpose(wT_ps[:, m, :], wsplit[:, m, :], ident_b[:])
         wT = const.tile([P, MT, P], BF16, name="wT")
-        widen_planes(0, (2, 4, 5, 6, 7))
-        nc.scalar.copy(out=wT[:], in_=wT_ps[:])
+        rsum_b = rsum[:].unsqueeze(2).to_broadcast([P, MT, NE])
+
+        widen(0, 0)
+        nc.vector.tensor_reduce(out=lmax[:], in_=logits[:], axis=AX.X, op=ALU.max)
+        widen(0, 3)
+        nc.vector.tensor_tensor(out=shifted[:], in0=logits[:], in1=lmax[:].unsqueeze(2).to_broadcast([P, MT, NE]), op=ALU.subtract)
+        widen(0, 2)
+        nc.scalar.activation(out=expd[:], in_=shifted[:], func=ACT.Exp)
+        widen(0, 1)
+        widen(0, 5)
+        nc.vector.tensor_reduce(out=esum[:], in_=expd[:], axis=AX.X, op=ALU.add)
+        widen(0, 4)
+        widen(0, 6)
+        nc.vector.reciprocal(out=rsum[:], in_=esum[:])
+        nc.vector.memset(wsplit[:], 0.0)
+        nc.vector.tensor_tensor(out=op_w[:], in0=expd[:], in1=rsum_b, op=ALU.mult)
+        nc.vector.tensor_tensor(out=wsplit[:, :, 0:NE], in0=expd[:], in1=rsum_b, op=ALU.mult)
+        widen(1, 2)
+        nc.vector.tensor_tensor(out=rest1[:], in0=op_w[:], in1=wsplit[:, :, 0:NE], op=ALU.subtract)
+        widen(1, 3)
+        nc.vector.tensor_copy(out=wsplit[:, :, NE : 2 * NE], in_=rest1[:])
+        widen(0, 7)
 
         xt = []
         bias_ps = []
@@ -218,10 +224,20 @@ def tile_enhancedmathematicalreasoning_pa_kernel(tc, hidden_states, op_logits, W
                 combine(c)
 
         transpose_hidden()
-        bias_products(0)
         for j in range(-2, NCH + 1):
             if 0 <= j + 1 < NCH:
                 interleave(j + 1, "S")
+            if j == -1:
+                nc.vector.tensor_tensor(out=rest2[:], in0=rest1[:], in1=wsplit[:, :, NE : 2 * NE], op=ALU.subtract)
+                widen(1, 6)
+                nc.vector.tensor_copy(out=wsplit[:, :, 2 * NE : 3 * NE], in_=rest2[:])
+                wT_ps = psum.tile([P, MT, P], BF16, name="bank")
+                for m in range(MT):
+                    nc.tensor.transpose(wT_ps[:, m, :], wsplit[:, m, :], ident_b[:])
+                widen(1, 4)
+                widen(1, 5)
+                nc.scalar.copy(out=wT[:], in_=wT_ps[:])
+                bias_products(0)
             widen_for_step(j)
             if 0 <= j + 1 < NCH:
                 interleave(j + 1, "V", (0,))

@@ -26,8 +26,10 @@ FLOPS = 2 * MT * P * K * NOUT * NE
 LAST_WIDTHS = (512, 256, 128, 128)
 CHUNKS = [(e, c0, 512) for e in range(NE - 1) for c0 in (0, 512)] + [(NE - 1, sum(LAST_WIDTHS[:i]), LAST_WIDTHS[i]) for i in range(len(LAST_WIDTHS))]
 NCH = len(CHUNKS)
-S_COLS = [64] * 12 + [224] * 2 + [320] * (NCH - 14)
-G_COLS = [192] * NCH
+S_COLS = [0] * 12 + [320] * (NCH - 12)
+G_COLS = [288] * 12 + [192] * (NCH - 12)
+P_COLS = [224] * 12 + [0] * (NCH - 12)
+EVAC_ON_S = ()
 V_PLANES = [(2, 3, 5, 6, 7), (2, 3, 6), (), (), (), (), (), ()]
 WIDE_BUFS = 3
 LAST_LEAD = 3
@@ -42,7 +44,8 @@ def tile_enhancedmathematicalreasoning_pa_kernel(tc, hidden_states, op_logits, W
         widep = ctx.enter_context(tc.tile_pool(name="widep", bufs=WIDE_BUFS))
         grp = ctx.enter_context(tc.tile_pool(name="grp", bufs=3))
         pair = ctx.enter_context(tc.tile_pool(name="pair", bufs=2))
-        psum = ctx.enter_context(tc.psum_pool(name="psum", bufs=8))
+        psum = ctx.enter_context(tc.psum_pool(name="psum", bufs=6))
+        psil = ctx.enter_context(tc.psum_pool(name="psil", bufs=2))
 
         warm = const.tile([P, 1], F32, name="warm")
         be3 = const.tile([P, NOUT], BF16, name="be3")
@@ -84,6 +87,7 @@ def tile_enhancedmathematicalreasoning_pa_kernel(tc, hidden_states, op_logits, W
         codes = {}
         scales = {}
         banks = {}
+        laid = {}
         widened = set()
 
         def widen(e, plane, c0=0, width=NOUT):
@@ -117,13 +121,41 @@ def tile_enhancedmathematicalreasoning_pa_kernel(tc, hidden_states, op_logits, W
             elif j + LAST_LEAD < NCH:
                 widen_planes(NE - 1, range(G * T), CHUNKS[j + LAST_LEAD][1], CHUNKS[j + LAST_LEAD][2])
 
+        def share(c, who):
+            width = CHUNKS[c][2]
+            g_cut = G_COLS[c] * width // 512
+            p_cut = width - P_COLS[c] * width // 512
+            s_cut = p_cut - S_COLS[c] * width // 512
+            return {"G": (0, g_cut), "V": (g_cut, s_cut), "S": (s_cut, p_cut), "P": (p_cut, width)}[who]
+
+        def pe_interleave(c):
+            e, c0, width = CHUNKS[c]
+            n0, n1 = share(c, "P")
+            if n0 >= n1:
+                return
+            laid[c] = []
+            pieces = -(-(n1 - n0) // P)
+            step = (n1 - n0) // pieces
+            for g in range(G):
+                laid[c].append(psil.tile([P, n1 - n0, T], BF16, name="laid"))
+                for a in range(n0, n1, step):
+                    nc.tensor.matmul(out=laid[c][g][:, a - n0 : a - n0 + step, :], lhsT=ident_b[:], rhs=wide[e][:, g, :, c0 + a : c0 + a + step].rearrange("p t n -> p n t"), start=True, stop=True)
+
+        def evacuate(c, who):
+            n0, n1 = share(c, "P")
+            if n0 >= n1 or (c in EVAC_ON_S) != (who == "S"):
+                return
+            for g in range(G):
+                if who == "S":
+                    nc.scalar.copy(out=grouped[c][:, g, n0:n1, :], in_=laid[c][g][:])
+                else:
+                    nc.vector.tensor_copy(out=grouped[c][:, g, n0:n1, :], in_=laid[c][g][:])
+
         def interleave(c, who, passes=(0, 1)):
             e, c0, width = CHUNKS[c]
             if c not in grouped:
                 grouped[c] = pair.tile([P, G, width, T], BF16, name="grouped", align_bytes=64)
-            g_cut = G_COLS[c] * width // 512
-            s_cut = width - S_COLS[c] * width // 512
-            n0, n1 = {"G": (0, g_cut), "V": (g_cut, s_cut), "S": (s_cut, width)}[who]
+            n0, n1 = share(c, who)
             if n0 >= n1:
                 return
             if who == "G":
@@ -144,10 +176,10 @@ def tile_enhancedmathematicalreasoning_pa_kernel(tc, hidden_states, op_logits, W
             scales[c] = grp.tile([P, G * width], U8, name="scales", align_bytes=64)
             nc.vector.quantize_mx(out=codes[c][:].bitcast(FP8X4), scales=scales[c][:], in_=grouped[c][:].rearrange("p g n t -> p (g n t)"))
 
-        def multiply(c):
+        def multiply(c, tiles):
             width = CHUNKS[c][2]
-            banks[c] = []
-            for m in range(MT):
+            banks.setdefault(c, [])
+            for m in tiles:
                 bank = psum.tile([P, width], F32, name="bank")
                 banks[c].append(bank)
                 for g in range(G):
@@ -156,9 +188,9 @@ def tile_enhancedmathematicalreasoning_pa_kernel(tc, hidden_states, op_logits, W
                     nc.tensor.matmul_mx(out=bank[:], lhsT=hcodes[:, tok].bitcast(FP8X4), lhsT_scale=hscales[:, tok],
                                         rhs=codes[c][:, col].bitcast(FP8X4), rhs_scale=scales[c][:, col], start=(g == 0), stop=(g == G - 1))
 
-        def combine(c):
+        def combine(c, tiles):
             e, c0, width = CHUNKS[c]
-            for m in range(MT):
+            for m in tiles:
                 part = acc[:, m, c0 : c0 + width]
                 nc.vector.scalar_tensor_tensor(out=part, in0=banks[c][m][:], scalar=op_w[:, m, e : e + 1], in1=part, op0=ALU.mult, op1=ALU.add)
                 if e == NE - 1:
@@ -206,27 +238,28 @@ def tile_enhancedmathematicalreasoning_pa_kernel(tc, hidden_states, op_logits, W
                     for u in range(2):
                         nc.tensor.transpose(xt[m][:, g, u, :], words[:, 256 * g + u : 256 * (g + 1) : 2], ident_f[:])
 
-        def bias_products(half):
-            for m in range(MT):
+        def bias_products(half, tiles):
+            for m in tiles:
                 bias_ps.append(psum.tile([P, 512], F32, name="bank"))
                 nc.tensor.matmul(out=bias_ps[half * MT + m][:], lhsT=wT[:, m, :], rhs=be3[:, half * 512 : (half + 1) * 512], start=True, stop=True)
 
-        def empty_banks(c):
+        def empty_banks(c, tiles):
             if c == -3:
-                for m in range(MT):
+                for m in tiles:
                     nc.vector.tensor_copy(out=hgrouped[:, :, m * P : (m + 1) * P, :].rearrange("p g r t -> p g (r t)").bitcast(F32).rearrange("p g (r u) -> p g r u", u=2),
                                           in_=xt[m][:].rearrange("p g u r -> p g r u"))
             elif c < 0:
                 half = c + 2
-                for m in range(MT):
+                for m in tiles:
                     nc.vector.tensor_copy(out=acc[:, m, half * 512 : (half + 1) * 512], in_=bias_ps[half * MT + m][:])
             else:
-                combine(c)
+                combine(c, tiles)
 
         transpose_hidden()
         for j in range(-2, NCH + 1):
             if 0 <= j + 1 < NCH:
                 interleave(j + 1, "S")
+                evacuate(j + 1, "S")
             if j == -1:
                 nc.vector.tensor_tensor(out=rest2[:], in0=rest1[:], in1=wsplit[:, :, NE : 2 * NE], op=ALU.subtract)
                 widen(1, 6)
@@ -237,18 +270,27 @@ def tile_enhancedmathematicalreasoning_pa_kernel(tc, hidden_states, op_logits, W
                 widen(1, 4)
                 widen(1, 5)
                 nc.scalar.copy(out=wT[:], in_=wT_ps[:])
-                bias_products(0)
+                bias_products(0, range(MT))
             widen_for_step(j)
             if 0 <= j + 1 < NCH:
                 interleave(j + 1, "V", (0,))
             if j == -1:
-                bias_products(1)
+                bias_products(1, (0, 1))
                 nc.vector.quantize_mx(out=hcodes[:].bitcast(FP8X4), scales=hscales[:], in_=hgrouped[:].rearrange("p g r t -> p (g r t)"))
             if 0 <= j < NCH:
                 quantize(j)
-                multiply(j)
+                multiply(j, (0, 1))
             if 0 <= j + 1 < NCH:
                 interleave(j + 1, "V", (1,))
             if j + 2 < NCH:
                 interleave(j + 2, "G")
-            empty_banks(j - 1)
+            if 0 <= j + 1 < NCH:
+                evacuate(j + 1, "V")
+            if 0 <= j + 2 < NCH:
+                pe_interleave(j + 2)
+            empty_banks(j - 1, (0, 1))
+            if j == -1:
+                bias_products(1, (2, 3))
+            if 0 <= j < NCH:
+                multiply(j, (2, 3))
+            empty_banks(j - 1, (2, 3))

@@ -26,14 +26,15 @@ FLOPS = 2 * MT * P * K * NOUT * NE
 LAST_WIDTHS = (512, 256, 128, 128)
 CHUNKS = [(e, c0, 512) for e in range(NE - 1) for c0 in (0, 512)] + [(NE - 1, sum(LAST_WIDTHS[:i]), LAST_WIDTHS[i]) for i in range(len(LAST_WIDTHS))]
 NCH = len(CHUNKS)
-S_COLS = [0] * 12 + [320] * (NCH - 12)
-G_COLS = [288] * 12 + [192] * (NCH - 12)
+S_COLS = [112] + [0] * 11 + [320] * (NCH - 12)
+G_COLS = [176] + [288] * 11 + [192] * (NCH - 12)
 P_COLS = [224] * 12 + [0] * (NCH - 12)
 EVAC_ON_S = ()
-V_PLANES = [(2, 3, 5, 6, 7), (2, 3, 6), (), (), (), (), (), ()]
+V_PLANES = [(1, 3, 5, 6, 7), (2, 3, 6), (), (), (), (), (), ()]
 WIDE_BUFS = 3
 LAST_LEAD = 3
-X_AFTER = 3
+X_AFTER = 4
+WT_BEHIND = (0, 1, 4)
 
 
 def tile_enhancedmathematicalreasoning_pa_kernel(tc, hidden_states, op_logits, We_bytes, We_scale, be, out):
@@ -52,6 +53,7 @@ def tile_enhancedmathematicalreasoning_pa_kernel(tc, hidden_states, op_logits, W
         wsplit = const.tile([P, MT, P], BF16, name="wsplit")
         nc.vector.memset(warm[:], 0.0)
         nc.vector.memset(be3[:], 0.0)
+        nc.vector.memset(wsplit[:], 0.0)
         nc.scalar.activation(out=warm[:], in_=warm[:], func=ACT.Exp)
         ident_f = const.tile([P, P], F32, name="ident_f")
         ident_b = const.tile([P, P], BF16, name="ident_b")
@@ -62,10 +64,10 @@ def tile_enhancedmathematicalreasoning_pa_kernel(tc, hidden_states, op_logits, W
         nc.sync.dma_start(out=wscale[:], in_=We_scale.rearrange("o (g p t) x -> p g (o t x)", p=P, t=T))
         wbytes = [const.tile([P, G, T, NOUT], U8, name="wbytes%d" % e) for e in range(NE)]
         wsrc = We_bytes.rearrange("e (g p t) n -> e g p t n", p=P, t=T)
-        for t in range(T):
-            nc.sync.dma_start(out=wbytes[0][:, 0, t, :], in_=wsrc[0, 0, :, t, :])
         logits = const.tile([P, MT, NE], BF16, name="logits")
         nc.sync.dma_start(out=logits[:], in_=op_logits.rearrange("b s e -> s b e"))
+        for t in range(T):
+            nc.sync.dma_start(out=wbytes[0][:, 0, t, :], in_=wsrc[0, 0, :, t, :])
         nc.sync.dma_start(out=wbytes[0][:, 1], in_=wsrc[0, 1])
         x_sb = [const.tile([P, K], BF16, name="x_sb%d" % m) for m in range(MT)]
         for i in range(2, 2 * NE):
@@ -206,26 +208,31 @@ def tile_enhancedmathematicalreasoning_pa_kernel(tc, hidden_states, op_logits, W
         wT = const.tile([P, MT, P], BF16, name="wT")
         rsum_b = rsum[:].unsqueeze(2).to_broadcast([P, MT, NE])
 
+        H = NOUT // 2
         widen(0, 0)
         nc.vector.tensor_reduce(out=lmax[:], in_=logits[:], axis=AX.X, op=ALU.max)
-        widen(0, 3)
-        nc.vector.tensor_tensor(out=shifted[:], in0=logits[:], in1=lmax[:].unsqueeze(2).to_broadcast([P, MT, NE]), op=ALU.subtract)
-        widen(0, 2)
-        nc.scalar.activation(out=expd[:], in_=shifted[:], func=ACT.Exp)
         widen(0, 1)
+        nc.vector.tensor_tensor(out=shifted[:], in0=logits[:], in1=lmax[:].unsqueeze(2).to_broadcast([P, MT, NE]), op=ALU.subtract)
+        widen(0, 3)
+        nc.scalar.activation(out=expd[:], in_=shifted[:], func=ACT.Exp)
+        widen(0, 2)
         widen(0, 5)
         nc.vector.tensor_reduce(out=esum[:], in_=expd[:], axis=AX.X, op=ALU.add)
         widen(0, 4)
         widen(0, 6)
         nc.vector.reciprocal(out=rsum[:], in_=esum[:])
-        nc.vector.memset(wsplit[:], 0.0)
+        widen(1, 2)
         nc.vector.tensor_tensor(out=op_w[:], in0=expd[:], in1=rsum_b, op=ALU.mult)
         nc.vector.tensor_tensor(out=wsplit[:, :, 0:NE], in0=expd[:], in1=rsum_b, op=ALU.mult)
-        widen(1, 2)
-        nc.vector.tensor_tensor(out=rest1[:], in0=op_w[:], in1=wsplit[:, :, 0:NE], op=ALU.subtract)
         widen(1, 3)
+        nc.vector.tensor_tensor(out=rest1[:], in0=op_w[:], in1=wsplit[:, :, 0:NE], op=ALU.subtract)
+        widen(1, 6, 0, H)
         nc.vector.tensor_copy(out=wsplit[:, :, NE : 2 * NE], in_=rest1[:])
-        widen(0, 7)
+        widen(1, 6, H, H)
+        nc.vector.tensor_tensor(out=rest2[:], in0=rest1[:], in1=wsplit[:, :, NE : 2 * NE], op=ALU.subtract)
+        widen(0, 7, 0, H)
+        nc.vector.tensor_copy(out=wsplit[:, :, 2 * NE : 3 * NE], in_=rest2[:])
+        widen(0, 7, H, H)
 
         xt = []
         bias_ps = []
@@ -256,20 +263,18 @@ def tile_enhancedmathematicalreasoning_pa_kernel(tc, hidden_states, op_logits, W
                 combine(c, tiles)
 
         transpose_hidden()
+        wT_ps = psum.tile([P, MT, P], BF16, name="bank")
+        for m in range(MT):
+            nc.tensor.transpose(wT_ps[:, m, :], wsplit[:, m, :], ident_b[:])
         for j in range(-2, NCH + 1):
             if 0 <= j + 1 < NCH:
                 interleave(j + 1, "S")
                 evacuate(j + 1, "S")
-            if j == -1:
-                nc.vector.tensor_tensor(out=rest2[:], in0=rest1[:], in1=wsplit[:, :, NE : 2 * NE], op=ALU.subtract)
-                widen(1, 6)
-                nc.vector.tensor_copy(out=wsplit[:, :, 2 * NE : 3 * NE], in_=rest2[:])
-                wT_ps = psum.tile([P, MT, P], BF16, name="bank")
-                for m in range(MT):
-                    nc.tensor.transpose(wT_ps[:, m, :], wsplit[:, m, :], ident_b[:])
-                widen(1, 4)
-                widen(1, 5)
+            if j == -2:
+                for plane in WT_BEHIND:
+                    widen(1, plane)
                 nc.scalar.copy(out=wT[:], in_=wT_ps[:])
+            if j == -1:
                 bias_products(0, range(MT))
             widen_for_step(j)
             if 0 <= j + 1 < NCH:

@@ -26,15 +26,15 @@ FLOPS = 2 * MT * P * K * NOUT * NE
 LAST_WIDTHS = (512, 256, 128, 128)
 CHUNKS = [(e, c0, 512) for e in range(NE - 1) for c0 in (0, 512)] + [(NE - 1, sum(LAST_WIDTHS[:i]), LAST_WIDTHS[i]) for i in range(len(LAST_WIDTHS))]
 NCH = len(CHUNKS)
-S_COLS = [112] + [0] * 11 + [320] * (NCH - 12)
-G_COLS = [176] + [288] * 11 + [192] * (NCH - 12)
+S_COLS = [64] + [0] * 11 + [320] * (NCH - 12)
+G_COLS = [224] + [288] * 11 + [192] * (NCH - 12)
 P_COLS = [224] * 12 + [0] * (NCH - 12)
 EVAC_ON_S = ()
-V_PLANES = [(1, 3, 5, 6, 7), (2, 3, 6), (), (), (), (), (), ()]
+V_PLANES = [(1, 3, 5, 6, 7), (3,), (), (), (), (), (), ()]
 WIDE_BUFS = 3
 LAST_LEAD = 3
-X_AFTER = 4
-WT_BEHIND = (0, 1, 4)
+X_AFTER = 3
+WT_BEHIND = (0, 1, 2)
 
 
 def tile_enhancedmathematicalreasoning_pa_kernel(tc, hidden_states, op_logits, We_bytes, We_scale, be, out):
@@ -216,23 +216,23 @@ def tile_enhancedmathematicalreasoning_pa_kernel(tc, hidden_states, op_logits, W
         widen(0, 3)
         nc.scalar.activation(out=expd[:], in_=shifted[:], func=ACT.Exp)
         widen(0, 2)
-        widen(0, 5)
+        widen(0, 5, 0, H)
+        widen(0, 5, H, H)
         nc.vector.tensor_reduce(out=esum[:], in_=expd[:], axis=AX.X, op=ALU.add)
         widen(0, 4)
-        widen(0, 6)
+        widen(0, 6, 0, H)
         nc.vector.reciprocal(out=rsum[:], in_=esum[:])
-        widen(1, 2)
+        widen(0, 6, H, H)
         nc.vector.tensor_tensor(out=op_w[:], in0=expd[:], in1=rsum_b, op=ALU.mult)
         nc.vector.tensor_tensor(out=wsplit[:, :, 0:NE], in0=expd[:], in1=rsum_b, op=ALU.mult)
-        widen(1, 3)
+        widen(1, 3, 0, H)
         nc.vector.tensor_tensor(out=rest1[:], in0=op_w[:], in1=wsplit[:, :, 0:NE], op=ALU.subtract)
-        widen(1, 6, 0, H)
+        widen(1, 3, H, H)
         nc.vector.tensor_copy(out=wsplit[:, :, NE : 2 * NE], in_=rest1[:])
-        widen(1, 6, H, H)
-        nc.vector.tensor_tensor(out=rest2[:], in0=rest1[:], in1=wsplit[:, :, NE : 2 * NE], op=ALU.subtract)
         widen(0, 7, 0, H)
-        nc.vector.tensor_copy(out=wsplit[:, :, 2 * NE : 3 * NE], in_=rest2[:])
+        nc.vector.tensor_tensor(out=rest2[:], in0=rest1[:], in1=wsplit[:, :, NE : 2 * NE], op=ALU.subtract)
         widen(0, 7, H, H)
+        nc.vector.tensor_copy(out=wsplit[:, :, 2 * NE : 3 * NE], in_=rest2[:])
 
         xt = []
         bias_ps = []

@@ -136,12 +136,10 @@ def tile_enhancedmathematicalreasoning_pa_kernel(tc, hidden_states, op_logits, W
             if n0 >= n1:
                 return
             laid[c] = []
-            pieces = -(-(n1 - n0) // P)
-            step = (n1 - n0) // pieces
             for g in range(G):
                 laid[c].append(psil.tile([P, n1 - n0, T], BF16, name="laid"))
-                for a in range(n0, n1, step):
-                    nc.tensor.matmul(out=laid[c][g][:, a - n0 : a - n0 + step, :], lhsT=ident_b[:], rhs=wide[e][:, g, :, c0 + a : c0 + a + step].rearrange("p t n -> p n t"), start=True, stop=True)
+                for v in range(T // 2):
+                    nc.tensor.matmul(out=laid[c][g][:, :, 2 * v : 2 * v + 2].rearrange("p n u -> p u n"), lhsT=ident_b[:], rhs=wide[e][:, g, 2 * v : 2 * v + 2, c0 + n0 : c0 + n1], start=True, stop=True)
 
         def evacuate(c, who):
             n0, n1 = share(c, "P")

@@ -27,7 +27,7 @@ LAST_WIDTHS = (512, 256, 128, 128)
 CHUNKS = [(e, c0, 512) for e in range(NE - 1) for c0 in (0, 512)] + [(NE - 1, sum(LAST_WIDTHS[:i]), LAST_WIDTHS[i]) for i in range(len(LAST_WIDTHS))]
 NCH = len(CHUNKS)
 S_COLS = [64] + [0] * 11 + [320] * (NCH - 12)
-G_COLS = [224] + [288] * 11 + [192] * (NCH - 12)
+G_COLS = [224] + [272] * 11 + [192] * (NCH - 12)
 P_COLS = [224] * 12 + [0] * (NCH - 12)
 EVAC_ON_S = ()
 V_PLANES = [(1, 3, 5, 6, 7), (3,), (), (), (), (), (), ()]
@@ -162,6 +162,9 @@ def tile_enhancedmathematicalreasoning_pa_kernel(tc, hidden_states, op_logits, W
                 src = wide[e][:, :, :, c0 + n0 : c0 + n1].rearrange("p g t n -> p g n t")
                 nc.gpsimd.tensor_scalar(out=grouped[c][:, :, n0:n1, :], in0=src, scalar1=1.0, scalar2=0.0, op0=ALU.mult, op1=ALU.add)
                 return
+            if who == "V":
+                nc.vector.tensor_copy(out=grouped[c][:, :, n0:n1, :], in_=wide[e][:, :, :, c0 + n0 : c0 + n1].rearrange("p g t n -> p g n t"))
+                return
             for g in passes:
                 src = wide[e][:, g, :, c0 + n0 : c0 + n1].rearrange("p t (c i) -> p c t i", i=4)
                 dst = grouped[c][:, g, n0:n1, :].rearrange("p (c i) t -> p c t i", i=4)
@@ -275,8 +278,6 @@ def tile_enhancedmathematicalreasoning_pa_kernel(tc, hidden_states, op_logits, W
             if j == -1:
                 bias_products(0, range(MT))
             widen_for_step(j)
-            if 0 <= j + 1 < NCH:
-                interleave(j + 1, "V", (0,))
             if j == -1:
                 bias_products(1, (0, 1))
                 nc.vector.quantize_mx(out=hcodes[:].bitcast(FP8X4), scales=hscales[:], in_=hgrouped[:].rearrange("p g r t -> p (g r t)"))
@@ -284,7 +285,7 @@ def tile_enhancedmathematicalreasoning_pa_kernel(tc, hidden_states, op_logits, W
                 quantize(j)
                 multiply(j, (0, 1))
             if 0 <= j + 1 < NCH:
-                interleave(j + 1, "V", (1,))
+                interleave(j + 1, "V")
             if j + 2 < NCH:
                 interleave(j + 2, "G")
             if 0 <= j + 1 < NCH:

@@ -28,7 +28,7 @@ CHUNKS = [(e, c0, 512) for e in range(NE - 1) for c0 in (0, 512)] + [(NE - 1, su
 NCH = len(CHUNKS)
 S_COLS = [64] + [0] * 11 + [320] * (NCH - 12)
 G_COLS = [224] + [272] * 11 + [192] * (NCH - 12)
-P_COLS = [224] * 12 + [0] * (NCH - 12)
+P_COLS = [224] + [192] * 11 + [0] * (NCH - 12)
 EVAC_ON_S = ()
 V_PLANES = [(1, 3, 5, 6, 7), (3,), (), (), (), (), (), ()]
 WIDE_BUFS = 3

@@ -26,10 +26,10 @@ FLOPS = 2 * MT * P * K * NOUT * NE
 LAST_WIDTHS = (512, 256, 128, 128)
 CHUNKS = [(e, c0, 512) for e in range(NE - 1) for c0 in (0, 512)] + [(NE - 1, sum(LAST_WIDTHS[:i]), LAST_WIDTHS[i]) for i in range(len(LAST_WIDTHS))]
 NCH = len(CHUNKS)
-S_COLS = [64] + [0] * 11 + [320] * (NCH - 12)
+S_COLS = [64] + [0] * 11 + [192] * (NCH - 12)
 G_COLS = [224] + [272] * 11 + [192] * (NCH - 12)
-P_COLS = [224] + [192] * 11 + [0] * (NCH - 12)
-EVAC_ON_S = ()
+P_COLS = [224] + [176] * 11 + [128] * (NCH - 12)
+EVAC_ON_S = tuple(range(12, NCH))
 V_PLANES = [(1, 3, 5, 6, 7), (3,), (), (), (), (), (), ()]
 WIDE_BUFS = 3
 LAST_LEAD = 3

@@ -130,13 +130,13 @@ def tile_enhancedmathematicalreasoning_pa_kernel(tc, hidden_states, op_logits, W
             s_cut = p_cut - S_COLS[c] * width // 512
             return {"G": (0, g_cut), "V": (g_cut, s_cut), "S": (s_cut, p_cut), "P": (p_cut, width)}[who]
 
-        def pe_interleave(c):
+        def pe_interleave(c, passes=(0, 1)):
             e, c0, width = CHUNKS[c]
             n0, n1 = share(c, "P")
             if n0 >= n1:
                 return
-            laid[c] = []
-            for g in range(G):
+            laid.setdefault(c, [])
+            for g in passes:
                 laid[c].append(psil.tile([P, n1 - n0, T], BF16, name="laid"))
                 for v in range(T // 2):
                     nc.tensor.matmul(out=laid[c][g][:, :, 2 * v : 2 * v + 2].rearrange("p n u -> p u n"), lhsT=ident_b[:], rhs=wide[e][:, g, 2 * v : 2 * v + 2, c0 + n0 : c0 + n1], start=True, stop=True)
@@ -263,6 +263,7 @@ def tile_enhancedmathematicalreasoning_pa_kernel(tc, hidden_states, op_logits, W
             else:
                 combine(c, tiles)
 
+        pe_interleave(0, (0,))
         transpose_hidden()
         wT_ps = psum.tile([P, MT, P], BF16, name="bank")
         for m in range(MT):
@@ -291,7 +292,7 @@ def tile_enhancedmathematicalreasoning_pa_kernel(tc, hidden_states, op_logits, W
             if 0 <= j + 1 < NCH:
                 evacuate(j + 1, "V")
             if 0 <= j + 2 < NCH:
-                pe_interleave(j + 2)
+                pe_interleave(j + 2, (1,) if j == -2 else (0, 1))
             empty_banks(j - 1, (0, 1))
             if j == -1:
                 bias_products(1, (2, 3))

@@ -23,7 +23,7 @@ NE = 8
 
 FLOPS = 2 * MT * P * K * NOUT * NE
 
-LAST_WIDTHS = (512, 256, 128, 128)
+LAST_WIDTHS = (256, 256, 256, 128, 128)
 CHUNKS = [(e, c0, 512) for e in range(NE - 1) for c0 in (0, 512)] + [(NE - 1, sum(LAST_WIDTHS[:i]), LAST_WIDTHS[i]) for i in range(len(LAST_WIDTHS))]
 NCH = len(CHUNKS)
 S_COLS = [64] + [0] * 11 + [192] * (NCH - 12)
@@ -31,9 +31,10 @@ G_COLS = [224] + [272] * 11 + [192] * (NCH - 12)
 P_COLS = [224] + [176] * 11 + [128] * (NCH - 12)
 EVAC_ON_S = tuple(range(12, NCH))
 V_PLANES = [(1, 3, 5, 6, 7), (3,), (), (), (), (), (), ()]
+FIRST_PLANES = (1, 0, 3, 2, 5, 4, 6, 7)
+SECOND_LOADS = [("w", 3), ("w", 0), ("x", 0), ("x", 1), ("x", 2), ("w", 1), ("x", 3), ("w", 2)]
 WIDE_BUFS = 3
 LAST_LEAD = 3
-X_AFTER = 3
 WT_BEHIND = (0, 1, 2)
 
 
@@ -66,16 +67,17 @@ def tile_enhancedmathematicalreasoning_pa_kernel(tc, hidden_states, op_logits, W
         wsrc = We_bytes.rearrange("e (g p t) n -> e g p t n", p=P, t=T)
         logits = const.tile([P, MT, NE], BF16, name="logits")
         nc.sync.dma_start(out=logits[:], in_=op_logits.rearrange("b s e -> s b e"))
-        for t in range(T):
-            nc.sync.dma_start(out=wbytes[0][:, 0, t, :], in_=wsrc[0, 0, :, t, :])
-        nc.sync.dma_start(out=wbytes[0][:, 1], in_=wsrc[0, 1])
+        for plane in FIRST_PLANES:
+            nc.sync.dma_start(out=wbytes[0][:, plane // T, plane % T, :], in_=wsrc[0, plane // T, :, plane % T, :])
         x_sb = [const.tile([P, K], BF16, name="x_sb%d" % m) for m in range(MT)]
-        for i in range(2, 2 * NE):
-            if i == X_AFTER:
-                for m in range(MT):
-                    nc.sync.dma_start(out=x_sb[m][:], in_=hidden_states[m])
-                for r in range(3):
-                    nc.sync.dma_start(out=be3[NE * r : NE * (r + 1), :], in_=be)
+        for what, i in SECOND_LOADS:
+            if what == "x":
+                nc.sync.dma_start(out=x_sb[i][:], in_=hidden_states[i])
+            else:
+                nc.sync.dma_start(out=wbytes[1][:, 0, i, :], in_=wsrc[1, 0, :, i, :])
+        for r in range(3):
+            nc.sync.dma_start(out=be3[NE * r : NE * (r + 1), :], in_=be)
+        for i in range(3, 2 * NE):
             nc.sync.dma_start(out=wbytes[i // 2][:, i % 2], in_=wsrc[i // 2, i % 2])
 
         acc = const.tile([P, MT, NOUT], F32, name="acc")
@@ -163,7 +165,7 @@ def tile_enhancedmathematicalreasoning_pa_kernel(tc, hidden_states, op_logits, W
                 nc.gpsimd.tensor_scalar(out=grouped[c][:, :, n0:n1, :], in0=src, scalar1=1.0, scalar2=0.0, op0=ALU.mult, op1=ALU.add)
                 return
             if who == "V":
-                nc.vector.tensor_copy(out=grouped[c][:, :, n0:n1, :], in_=wide[e][:, :, :, c0 + n0 : c0 + n1].rearrange("p g t n -> p g n t"))
+                nc.vector.tensor_copy(out=grouped[c][:, :, n0:n1, :].rearrange("p g (c i) t -> p g c t i", i=4), in_=wide[e][:, :, :, c0 + n0 : c0 + n1].rearrange("p g t (c i) -> p g c t i", i=4))
                 return
             for g in passes:
                 src = wide[e][:, g, :, c0 + n0 : c0 + n1].rearrange("p t (c i) -> p c t i", i=4)
@@ -205,7 +207,6 @@ def tile_enhancedmathematicalreasoning_pa_kernel(tc, hidden_states, op_logits, W
         esum = const.tile([P, MT], F32, name="esum")
         rsum = const.tile([P, MT], F32, name="rsum")
         rest1 = const.tile([P, MT, NE], F32, name="rest1")
-        rest2 = const.tile([P, MT, NE], F32, name="rest2")
         wT = const.tile([P, MT, P], BF16, name="wT")
         rsum_b = rsum[:].unsqueeze(2).to_broadcast([P, MT, NE])
 
@@ -226,14 +227,13 @@ def tile_enhancedmathematicalreasoning_pa_kernel(tc, hidden_states, op_logits, W
         widen(0, 6, H, H)
         nc.vector.tensor_tensor(out=op_w[:], in0=expd[:], in1=rsum_b, op=ALU.mult)
         nc.vector.tensor_tensor(out=wsplit[:, :, 0:NE], in0=expd[:], in1=rsum_b, op=ALU.mult)
-        widen(1, 3, 0, H)
+        widen(0, 7, H, H)
         nc.vector.tensor_tensor(out=rest1[:], in0=op_w[:], in1=wsplit[:, :, 0:NE], op=ALU.subtract)
-        widen(1, 3, H, H)
+        widen(1, 3, 0, H)
         nc.vector.tensor_copy(out=wsplit[:, :, NE : 2 * NE], in_=rest1[:])
         widen(0, 7, 0, H)
-        nc.vector.tensor_tensor(out=rest2[:], in0=rest1[:], in1=wsplit[:, :, NE : 2 * NE], op=ALU.subtract)
-        widen(0, 7, H, H)
-        nc.vector.tensor_copy(out=wsplit[:, :, 2 * NE : 3 * NE], in_=rest2[:])
+        nc.vector.tensor_tensor(out=wsplit[:, :, 2 * NE : 3 * NE], in0=rest1[:], in1=wsplit[:, :, NE : 2 * NE], op=ALU.subtract)
+        widen(1, 3, H, H)
 
         xt = []
         bias_ps = []

@@ -26,9 +26,9 @@ FLOPS = 2 * MT * P * K * NOUT * NE
 LAST_WIDTHS = (256, 256, 256, 128, 128)
 CHUNKS = [(e, c0, 512) for e in range(NE - 1) for c0 in (0, 512)] + [(NE - 1, sum(LAST_WIDTHS[:i]), LAST_WIDTHS[i]) for i in range(len(LAST_WIDTHS))]
 NCH = len(CHUNKS)
-S_COLS = [64] + [0] * 11 + [192] * (NCH - 12)
-G_COLS = [224] + [272] * 11 + [192] * (NCH - 12)
-P_COLS = [224] + [176] * 11 + [128] * (NCH - 12)
+S_COLS = [64] + [8] * 11 + [224] * (NCH - 12)
+G_COLS = [224] + [276] * 11 + [192] * (NCH - 12)
+P_COLS = [224] + [192] * 11 + [96] * (NCH - 12)
 EVAC_ON_S = tuple(range(12, NCH))
 V_PLANES = [(1, 3, 5, 6, 7), (3,), (), (), (), (), (), ()]
 FIRST_PLANES = (1, 0, 3, 2, 5, 4, 6, 7)

@@ -26,9 +26,9 @@ FLOPS = 2 * MT * P * K * NOUT * NE
 LAST_WIDTHS = (256, 256, 256, 128, 128)
 CHUNKS = [(e, c0, 512) for e in range(NE - 1) for c0 in (0, 512)] + [(NE - 1, sum(LAST_WIDTHS[:i]), LAST_WIDTHS[i]) for i in range(len(LAST_WIDTHS))]
 NCH = len(CHUNKS)
-S_COLS = [64] + [8] * 11 + [224] * (NCH - 12)
+S_COLS = [64] + [36 * (c % 3 == 2) for c in range(1, 12)] + [232] * (NCH - 14) + [320, 320]
 G_COLS = [224] + [276] * 11 + [192] * (NCH - 12)
-P_COLS = [224] + [192] * 11 + [96] * (NCH - 12)
+P_COLS = [224] + [200] * 11 + [88] * (NCH - 14) + [0, 0]
 EVAC_ON_S = tuple(range(12, NCH))
 V_PLANES = [(1, 3, 5, 6, 7), (3,), (), (), (), (), (), ()]
 FIRST_PLANES = (1, 0, 3, 2, 5, 4, 6, 7)
@@ -66,9 +66,10 @@ def tile_enhancedmathematicalreasoning_pa_kernel(tc, hidden_states, op_logits, W
         wbytes = [const.tile([P, G, T, NOUT], U8, name="wbytes%d" % e) for e in range(NE)]
         wsrc = We_bytes.rearrange("e (g p t) n -> e g p t n", p=P, t=T)
         logits = const.tile([P, MT, NE], BF16, name="logits")
-        nc.sync.dma_start(out=logits[:], in_=op_logits.rearrange("b s e -> s b e"))
         for plane in FIRST_PLANES:
             nc.sync.dma_start(out=wbytes[0][:, plane // T, plane % T, :], in_=wsrc[0, plane // T, :, plane % T, :])
+            if plane == FIRST_PLANES[1]:
+                nc.sync.dma_start(out=logits[:], in_=op_logits.rearrange("b s e -> s b e"))
         x_sb = [const.tile([P, K], BF16, name="x_sb%d" % m) for m in range(MT)]
         for what, i in SECOND_LOADS:
             if what == "x":
@@ -212,10 +213,11 @@ def tile_enhancedmathematicalreasoning_pa_kernel(tc, hidden_states, op_logits, W
 
         H = NOUT // 2
         widen(0, 0)
-        nc.vector.tensor_reduce(out=lmax[:], in_=logits[:], axis=AX.X, op=ALU.max)
         widen(0, 1)
+        nc.vector.tensor_reduce(out=lmax[:], in_=logits[:], axis=AX.X, op=ALU.max)
+        widen(0, 3, 0, H)
         nc.vector.tensor_tensor(out=shifted[:], in0=logits[:], in1=lmax[:].unsqueeze(2).to_broadcast([P, MT, NE]), op=ALU.subtract)
-        widen(0, 3)
+        widen(0, 3, H, H)
         nc.scalar.activation(out=expd[:], in_=shifted[:], func=ACT.Exp)
         widen(0, 2)
         widen(0, 5, 0, H)

from contextlib import ExitStack

import concourse.mybir as mybir
from concourse.masks import make_identity

F32 = mybir.dt.float32
BF16 = mybir.dt.bfloat16
U32 = mybir.dt.uint32
U8 = mybir.dt.uint8
FP8 = mybir.dt.float8_e4m3fn
FP8X4 = mybir.dt.float8_e4m3fn_x4
ACT = mybir.ActivationFunctionType
ALU = mybir.AluOpType
AX = mybir.AxisListType

P = 128
MT = 4
K = 1024
G = 2
T = 4
NOUT = 1024
NE = 8

FLOPS = 2 * MT * P * K * NOUT * NE

LAST_WIDTHS = (256, 256, 256, 128, 128)
CHUNKS = [(e, c0, 512) for e in range(NE - 1) for c0 in (0, 512)] + [(NE - 1, sum(LAST_WIDTHS[:i]), LAST_WIDTHS[i]) for i in range(len(LAST_WIDTHS))]
NCH = len(CHUNKS)
S_COLS = [64] + [36 * (c % 3 == 2) for c in range(1, 12)] + [232] * (NCH - 14) + [320, 320]
G_COLS = [224] + [276] * 11 + [192] * (NCH - 12)
P_COLS = [224] + [200] * 11 + [88] * (NCH - 14) + [0, 0]
EVAC_ON_S = tuple(range(12, NCH))
V_PLANES = [(1, 3, 5, 6, 7), (3,), (), (), (), (), (), ()]
FIRST_PLANES = (1, 0, 3, 2, 5, 4, 6, 7)
SECOND_LOADS = [("w", 3), ("w", 0), ("x", 0), ("x", 1), ("x", 2), ("w", 1), ("x", 3), ("w", 2)]
WIDE_BUFS = 3
LAST_LEAD = 3
WT_BEHIND = (0, 1, 2)


def tile_enhancedmathematicalreasoning_pa_kernel(tc, hidden_states, op_logits, We_bytes, We_scale, be, out):
    nc = tc.nc
    with ExitStack() as ctx:
        ctx.enter_context(tc.manual_schedule())
        const = ctx.enter_context(tc.tile_pool(name="const", bufs=1))
        widep = ctx.enter_context(tc.tile_pool(name="widep", bufs=WIDE_BUFS))
        grp = ctx.enter_context(tc.tile_pool(name="grp", bufs=3))
        pair = ctx.enter_context(tc.tile_pool(name="pair", bufs=2))
        psum = ctx.enter_context(tc.psum_pool(name="psum", bufs=6))
        psil = ctx.enter_context(tc.psum_pool(name="psil", bufs=2))

        warm = const.tile([P, 1], F32, name="warm")
        be3 = const.tile([P, NOUT], BF16, name="be3")
        wsplit = const.tile([P, MT, P], BF16, name="wsplit")
        nc.vector.memset(warm[:], 0.0)
        nc.vector.memset(be3[:], 0.0)
        nc.vector.memset(wsplit[:], 0.0)
        nc.scalar.activation(out=warm[:], in_=warm[:], func=ACT.Exp)
        ident_f = const.tile([P, P], F32, name="ident_f")
        ident_b = const.tile([P, P], BF16, name="ident_b")
        make_identity(nc, ident_f[:])
        make_identity(nc, ident_b[:])

        wscale = const.tile([P, G, T], F32, name="wscale")
        nc.sync.dma_start(out=wscale[:], in_=We_scale.rearrange("o (g p t) x -> p g (o t x)", p=P, t=T))
        wbytes = [const.tile([P, G, T, NOUT], U8, name="wbytes%d" % e) for e in range(NE)]
        wsrc = We_bytes.rearrange("e (g p t) n -> e g p t n", p=P, t=T)
        logits = const.tile([P, MT, NE], BF16, name="logits")
        for plane in FIRST_PLANES:
            nc.sync.dma_start(out=wbytes[0][:, plane // T, plane % T, :], in_=wsrc[0, plane // T, :, plane % T, :])
            if plane == FIRST_PLANES[1]:
                nc.sync.dma_start(out=logits[:], in_=op_logits.rearrange("b s e -> s b e"))
        x_sb = [const.tile([P, K], BF16, name="x_sb%d" % m) for m in range(MT)]
        for what, i in SECOND_LOADS:
            if what == "x":
                nc.sync.dma_start(out=x_sb[i][:], in_=hidden_states[i])
            else:
                nc.sync.dma_start(out=wbytes[1][:, 0, i, :], in_=wsrc[1, 0, :, i, :])
        for r in range(3):
            nc.sync.dma_start(out=be3[NE * r : NE * (r + 1), :], in_=be)
        for i in range(3, 2 * NE):
            nc.sync.dma_start(out=wbytes[i // 2][:, i % 2], in_=wsrc[i // 2, i % 2])

        acc = const.tile([P, MT, NOUT], F32, name="acc")
        op_w = const.tile([P, MT, NE], F32, name="op_w")
        hgrouped = pair.tile([P, G, MT * P, T], BF16, name="grouped", align_bytes=64)
        hcodes = const.tile([P, G * MT * P], U32, name="hcodes", align_bytes=64)
        hscales = const.tile([P, G * MT * P], U8, name="hscales", align_bytes=64)

        wide = {}
        grouped = {}
        codes = {}
        scales = {}
        banks = {}
        laid = {}
        widened = set()

        def widen(e, plane, c0=0, width=NOUT):
            if (e, plane, c0) in widened:
                return
            widened.add((e, plane, c0))
            if e not in wide:
                wide[e] = widep.tile([P, G, T, NOUT], BF16, name="wide")
            g, t = divmod(plane, T)
            src = wbytes[e][:, g, t, c0 : c0 + width].bitcast(FP8)
            if plane in V_PLANES[e]:
                nc.vector.tensor_scalar(out=wide[e][:, g, t, c0 : c0 + width], in0=src, scalar1=wscale[:, g, t : t + 1], scalar2=None, op0=ALU.mult)
            else:
                nc.scalar.activation(out=wide[e][:, g, t, c0 : c0 + width], in_=src, func=ACT.Copy, scale=wscale[:, g, t : t + 1])

        def widen_planes(e, planes, c0=0, width=NOUT):
            for plane in planes:
                if plane not in V_PLANES[e]:
                    widen(e, plane, c0, width)
            for plane in planes:
                if plane in V_PLANES[e]:
                    widen(e, plane, c0, width)

        def widen_for_step(j):
            e = (j + 4) // 2
            half = range(T * (j % 2), T * (j % 2) + T)
            if 1 <= e < NE - 1:
                widen_planes(e, half)
            elif e == NE - 1:
                widen_planes(e, half, 0, LAST_WIDTHS[0])
            elif j + LAST_LEAD < NCH:
                widen_planes(NE - 1, range(G * T), CHUNKS[j + LAST_LEAD][1], CHUNKS[j + LAST_LEAD][2])

        def share(c, who):
            width = CHUNKS[c][2]
            g_cut = G_COLS[c] * width // 512
            p_cut = width - P_COLS[c] * width // 512
            s_cut = p_cut - S_COLS[c] * width // 512
            return {"G": (0, g_cut), "V": (g_cut, s_cut), "S": (s_cut, p_cut), "P": (p_cut, width)}[who]

        def pe_interleave(c, passes=(0, 1)):
            e, c0, width = CHUNKS[c]
            n0, n1 = share(c, "P")
            if n0 >= n1:
                return
            laid.setdefault(c, [])
            for g in passes:
                laid[c].append(psil.tile([P, n1 - n0, T], BF16, name="laid"))
                for v in range(T // 2):
                    nc.tensor.matmul(out=laid[c][g][:, :, 2 * v : 2 * v + 2].rearrange("p n u -> p u n"), lhsT=ident_b[:], rhs=wide[e][:, g, 2 * v : 2 * v + 2, c0 + n0 : c0 + n1], start=True, stop=True)

        def evacuate(c, who):
            n0, n1 = share(c, "P")
            if n0 >= n1 or (c in EVAC_ON_S) != (who == "S"):
                return
            for g in range(G):
                if who == "S":
                    nc.scalar.copy(out=grouped[c][:, g, n0:n1, :], in_=laid[c][g][:])
                else:
                    nc.vector.tensor_copy(out=grouped[c][:, g, n0:n1, :], in_=laid[c][g][:])

        def interleave(c, who, passes=(0, 1)):
            e, c0, width = CHUNKS[c]
            if c not in grouped:
                grouped[c] = pair.tile([P, G, width, T], BF16, name="grouped", align_bytes=64)
            n0, n1 = share(c, who)
            if n0 >= n1:
                return
            if who == "G":
                src = wide[e][:, :, :, c0 + n0 : c0 + n1].rearrange("p g t n -> p g n t")
                nc.gpsimd.tensor_scalar(out=grouped[c][:, :, n0:n1, :], in0=src, scalar1=1.0, scalar2=0.0, op0=ALU.mult, op1=ALU.add)
                return
            if who == "V":
                nc.vector.tensor_copy(out=grouped[c][:, :, n0:n1, :].rearrange("p g (c i) t -> p g c t i", i=4), in_=wide[e][:, :, :, c0 + n0 : c0 + n1].rearrange("p g t (c i) -> p g c t i", i=4))
                return
            for g in passes:
                src = wide[e][:, g, :, c0 + n0 : c0 + n1].rearrange("p t (c i) -> p c t i", i=4)
                dst = grouped[c][:, g, n0:n1, :].rearrange("p (c i) t -> p c t i", i=4)
                if who == "V":
                    nc.vector.tensor_copy(out=dst, in_=src)
                else:
                    nc.scalar.copy(out=dst, in_=src)

        def quantize(c):
            width = CHUNKS[c][2]
            codes[c] = grp.tile([P, G * width], U32, name="codes", align_bytes=64)
            scales[c] = grp.tile([P, G * width], U8, name="scales", align_bytes=64)
            nc.vector.quantize_mx(out=codes[c][:].bitcast(FP8X4), scales=scales[c][:], in_=grouped[c][:].rearrange("p g n t -> p (g n t)"))

        def multiply(c, tiles):
            width = CHUNKS[c][2]
            banks.setdefault(c, [])
            for m in tiles:
                bank = psum.tile([P, width], F32, name="bank")
                banks[c].append(bank)
                for g in range(G):
                    tok = slice(g * MT * P + m * P, g * MT * P + (m + 1) * P)
                    col = slice(g * width, (g + 1) * width)
                    nc.tensor.matmul_mx(out=bank[:], lhsT=hcodes[:, tok].bitcast(FP8X4), lhsT_scale=hscales[:, tok],
                                        rhs=codes[c][:, col].bitcast(FP8X4), rhs_scale=scales[c][:, col], start=(g == 0), stop=(g == G - 1))

        def combine(c, tiles):
            e, c0, width = CHUNKS[c]
            for m in tiles:
                part = acc[:, m, c0 : c0 + width]
                nc.vector.scalar_tensor_tensor(out=part, in0=banks[c][m][:], scalar=op_w[:, m, e : e + 1], in1=part, op0=ALU.mult, op1=ALU.add)
                if e == NE - 1:
                    nc.sync.dma_start(out=out[m, :, c0 : c0 + width], in_=part)

        lmax = const.tile([P, MT], F32, name="lmax")
        shifted = const.tile([P, MT, NE], F32, name="shifted")
        expd = const.tile([P, MT, NE], F32, name="expd")
        esum = const.tile([P, MT], F32, name="esum")
        rsum = const.tile([P, MT], F32, name="rsum")
        rest1 = const.tile([P, MT, NE], F32, name="rest1")
        wT = const.tile([P, MT, P], BF16, name="wT")
        rsum_b = rsum[:].unsqueeze(2).to_broadcast([P, MT, NE])

        H = NOUT // 2
        widen(0, 0)
        widen(0, 1)
        nc.vector.tensor_reduce(out=lmax[:], in_=logits[:], axis=AX.X, op=ALU.max)
        widen(0, 3, 0, H)
        nc.vector.tensor_tensor(out=shifted[:], in0=logits[:], in1=lmax[:].unsqueeze(2).to_broadcast([P, MT, NE]), op=ALU.subtract)
        widen(0, 3, H, H)
        nc.scalar.activation(out=expd[:], in_=shifted[:], func=ACT.Exp)
        widen(0, 2)
        widen(0, 5, 0, H)
        widen(0, 5, H, H)
        nc.vector.tensor_reduce(out=esum[:], in_=expd[:], axis=AX.X, op=ALU.add)
        widen(0, 4)
        widen(0, 6, 0, H)
        nc.vector.reciprocal(out=rsum[:], in_=esum[:])
        widen(0, 6, H, H)
        nc.vector.tensor_tensor(out=op_w[:], in0=expd[:], in1=rsum_b, op=ALU.mult)
        nc.vector.tensor_tensor(out=wsplit[:, :, 0:NE], in0=expd[:], in1=rsum_b, op=ALU.mult)
        widen(0, 7, H, H)
        nc.vector.tensor_tensor(out=rest1[:], in0=op_w[:], in1=wsplit[:, :, 0:NE], op=ALU.subtract)
        widen(1, 3, 0, H)
        nc.vector.tensor_copy(out=wsplit[:, :, NE : 2 * NE], in_=rest1[:])
        widen(0, 7, 0, H)
        nc.vector.tensor_tensor(out=wsplit[:, :, 2 * NE : 3 * NE], in0=rest1[:], in1=wsplit[:, :, NE : 2 * NE], op=ALU.subtract)
        widen(1, 3, H, H)

        xt = []
        bias_ps = []

        def transpose_hidden():
            for m in range(MT):
                xt.append(psum.tile([P, G, 2, P], F32, name="bank"))
                words = x_sb[m][:].bitcast(F32)
                for g in range(G):
                    for u in range(2):
                        nc.tensor.transpose(xt[m][:, g, u, :], words[:, 256 * g + u : 256 * (g + 1) : 2], ident_f[:])

        def bias_products(half, tiles):
            for m in tiles:
                bias_ps.append(psum.tile([P, 512], F32, name="bank"))
                nc.tensor.matmul(out=bias_ps[half * MT + m][:], lhsT=wT[:, m, :], rhs=be3[:, half * 512 : (half + 1) * 512], start=True, stop=True)

        def empty_banks(c, tiles):
            if c == -3:
                for m in tiles:
                    nc.vector.tensor_copy(out=hgrouped[:, :, m * P : (m + 1) * P, :].rearrange("p g r t -> p g (r t)").bitcast(F32).rearrange("p g (r u) -> p g r u", u=2),
                                          in_=xt[m][:].rearrange("p g u r -> p g r u"))
            elif c < 0:
                half = c + 2
                for m in tiles:
                    nc.vector.tensor_copy(out=acc[:, m, half * 512 : (half + 1) * 512], in_=bias_ps[half * MT + m][:])
            else:
                combine(c, tiles)

        pe_interleave(0, (0,))
        transpose_hidden()
        wT_ps = psum.tile([P, MT, P], BF16, name="bank")
        for m in range(MT):
            nc.tensor.transpose(wT_ps[:, m, :], wsplit[:, m, :], ident_b[:])
        for j in range(-2, NCH + 1):
            if 0 <= j + 1 < NCH:
                interleave(j + 1, "S")
                evacuate(j + 1, "S")
            if j == -2:
                for plane in WT_BEHIND:
                    widen(1, plane)
                nc.scalar.copy(out=wT[:], in_=wT_ps[:])
            if j == -1:
                bias_products(0, range(MT))
            widen_for_step(j)
            if j == -1:
                bias_products(1, (0, 1))
                nc.vector.quantize_mx(out=hcodes[:].bitcast(FP8X4), scales=hscales[:], in_=hgrouped[:].rearrange("p g r t -> p (g r t)"))
            if 0 <= j < NCH:
                quantize(j)
                multiply(j, (0, 1))
            if 0 <= j + 1 < NCH:
                interleave(j + 1, "V")
            if j + 2 < NCH:
                interleave(j + 2, "G")
            if 0 <= j + 1 < NCH:
                evacuate(j + 1, "V")
            if 0 <= j + 2 < NCH:
                pe_interleave(j + 2, (1,) if j == -2 else (0, 1))
            empty_banks(j - 1, (0, 1))
            if j == -1:
                bias_products(1, (2, 3))
            if 0 <= j < NCH:
                multiply(j, (2, 3))
            empty_banks(j - 1, (2, 3))
